import numpy as np
import ml_dtypes


def mxq(x, axis, fmt="e4m3"):
    dtype, down = {"e4m3": (ml_dtypes.float8_e4m3fn, 7), "e5m2": (ml_dtypes.float8_e5m2, 14)}[fmt]
    v = np.moveaxis(np.asarray(x, np.float32).astype(ml_dtypes.bfloat16).astype(np.float64), axis, -1)
    blocks = v.reshape(v.shape[:-1] + (-1, 32))
    amax = np.abs(blocks).max(-1, keepdims=True)
    byte = np.maximum(np.where(amax > 0, np.frexp(amax)[1] - 1 + 127, 0) - down, 1)
    scale = np.exp2(byte - 127.0)
    codes = (blocks / scale).astype(np.float32).astype(dtype).astype(np.float64)
    return np.moveaxis((codes * scale).reshape(v.shape), -1, axis)


WIDE = False


def mx_kscale(k):
    if not WIDE:
        return np.ones(k)
    levels = np.array([30, -30])
    if k % 512:
        return np.exp2(np.random.permutation(np.resize(levels, k // 32))).repeat(32)
    a = np.empty((k // 512, 16))
    for p in range(k // 512):
        a[p, :8] = np.random.permutation(np.resize(levels, 8))
        for g in range(8):
            far = levels[np.abs(levels - a[p, g]) >= 10]
            a[p, g + 8] = far[np.random.randint(len(far))]
    return np.exp2(a.ravel()).repeat(32)


BF16 = ml_dtypes.bfloat16


def bf(x):
    return np.asarray(x, np.float32).astype(BF16)


def f64(x):
    return np.asarray(x).astype(np.float64)


E2M1 = np.array([0.0, 0.5, 1.0, 1.5, 2.0, 3.0, 4.0, 6.0, -0.0, -0.5, -1.0, -1.5, -2.0, -3.0, -4.0, -6.0])


def pack_weight(w, fmt):
    k, n = w.shape
    w = f64(bf(w)).reshape(k // 32, 32, n)
    amax = np.abs(w).max(1)
    if fmt == "e4m3":
        byte = np.frexp(amax)[1] - 1 + 127 - 7
    else:
        mant, ex = np.frexp(amax / 6.0)
        byte = np.where(mant > 0.5, ex, ex - 1) + 127
    byte = np.clip(np.where(amax > 0, byte, 1), 1, 254)
    scaled = (w * np.exp2(127.0 - byte)[:, None, :]).reshape(k, n).astype(np.float32)
    by_word = np.ascontiguousarray(scaled.reshape(k // 512, 128, 4, n).transpose(0, 1, 3, 2))
    if fmt == "e4m3":
        words = by_word.astype(ml_dtypes.float8_e4m3fn).view(np.uint8)
    else:
        c = by_word.astype(ml_dtypes.float4_e2m1fn).view(np.uint8) & 0xF
        words = c[..., 0::2] | (c[..., 1::2] << 4)
    return np.ascontiguousarray(words), np.ascontiguousarray(byte.astype(np.uint8).reshape(k // 512, 16, n))


def unpack_weight(words, scales, fmt):
    g, p, n, _ = words.shape
    if fmt == "e4m3":
        vals = np.ascontiguousarray(words).view(ml_dtypes.float8_e4m3fn).astype(np.float64)
    else:
        nib = np.empty((g, p, n, 4), np.uint8)
        nib[..., 0::2] = words & 0xF
        nib[..., 1::2] = words >> 4
        vals = E2M1[nib]
    vals = vals * np.repeat(np.exp2(scales.astype(np.float64) - 127.0), 8, axis=1)[..., None]
    return vals.transpose(0, 1, 3, 2).reshape(g * 512, n)

def pack4(w):
    words, scales = pack_weight(w, "e2m1")
    return words.reshape(words.shape[0], 128, -1), scales


def unpack4(words, scales):
    return unpack_weight(words.reshape(words.shape[0], 128, -1, 2), scales, "e2m1")


B, D, H = 1024, 512, 1024


def sigmoid(v):
    return 1.0 / (1.0 + np.exp(-v))


def setup_inputs():
    s = mx_kscale(D)
    x = bf(np.random.standard_normal((B, D)) * s)
    w = np.random.standard_normal((4 * H, D)) * 1.5 / np.sqrt(D) / s[None, :]
    words, scales = pack4(np.ascontiguousarray(w.T))
    b_ih0 = bf(np.random.standard_normal(4 * H) * 0.3)
    b_hh0 = bf(np.random.standard_normal(4 * H) * 0.3)
    return {"x": x,
            "W_ih0_words": words,
            "W_ih0_scales": scales,
            "b_ih0": b_ih0,
            "b_hh0": b_hh0}


def reference(x, W_ih0_words, W_ih0_scales, b_ih0, b_hh0):
    wt = unpack4(W_ih0_words, W_ih0_scales)
    b = f64(b_ih0) + f64(b_hh0)
    xq = mxq(f64(x), 1, "e5m2")
    a_i = (xq @ wt[:, :H]) + b[:H]
    a_go = (xq @ wt[:, 2 * H:]) + b[2 * H:]
    a_g, a_o = a_go[:, :H], a_go[:, H:]
    c = sigmoid(a_i) * np.tanh(a_g)
    return sigmoid(a_o) * np.tanh(c)

@@ -1,0 +1,214 @@
+from contextlib import ExitStack
+
+import concourse.mybir as mybir
+from concourse.masks import make_identity
+
+B, D, H = 1024, 512, 1024
+FLOPS = 2 * B * D * 3 * H
+BYTES = B * D * 2 + 3 * H * (D // 2 + D // 32) + 2 * 3 * H * 2 + B * H * 4
+
+F32 = mybir.dt.float32
+BF16 = mybir.dt.bfloat16
+I32 = mybir.dt.int32
+U32 = mybir.dt.uint32
+U8 = mybir.dt.uint8
+E5M2X4 = mybir.dt.float8_e5m2_x4
+E2M1X4 = mybir.dt.float4_e2m1fn_x4
+ACT = mybir.ActivationFunctionType
+ALU = mybir.AluOpType
+
+P = 128
+BANK = 512
+TILES = H // P
+GATE_I, GATE_G, GATE_O = 0, 1, 2
+EARLY = 2
+
+
+def tile_lstmbaseline_pa_kernel(tc, x, W_ih0_words, W_ih0_scales, b_ih0, b_hh0, out):
+    nc = tc.nc
+
+    units = [(0, 0, P), (1, 0, 2 * P), (0, P, 3 * P), (1, 2 * P, 2 * P)]
+    units += [(j, 0, BANK) for j in range(EARLY, TILES)] + [(j, BANK, BANK) for j in range(TILES)]
+    last = len(units) - 1
+
+    with ExitStack() as ctx:
+        keep = ctx.enter_context(tc.tile_pool(name="keep", bufs=1))
+        work = ctx.enter_context(tc.tile_pool(name="work", bufs=3))
+        gate_psum = ctx.enter_context(tc.psum_pool(name="gate_psum", bufs=4))
+        turn_psum = ctx.enter_context(tc.psum_pool(name="turn_psum", bufs=4))
+        ctx.enter_context(tc.manual_schedule())
+
+        ident = keep.tile([P, P], F32, align_bytes=64)
+        pick = keep.tile([P, TILES], BF16, align_bytes=64)
+        bias_rows = keep.tile([P, 3, P], BF16, align_bytes=64)
+        bias_ig = keep.tile([P, 2, TILES], F32, align_bytes=64)
+        bias_o = keep.tile([P, 1, TILES], F32, align_bytes=64)
+        w_ig_early = keep.tile([P, 2, 2 * P * EARLY], U8, align_bytes=64)
+        w_ig_late = keep.tile([P, 2, 2 * P * (TILES - EARLY)], U8, align_bytes=64)
+        w_o = keep.tile([P, 2 * H], U8, align_bytes=64)
+        ws_ig = keep.tile([P, 2, H], U8, align_bytes=64)
+        ws_o = keep.tile([P, H], U8, align_bytes=64)
+        x_codes = keep.tile([P, B], U32, align_bytes=64)
+        x_scales = keep.tile([P, B], U8, align_bytes=64)
+
+        chunks = [(0, 1), (1, 1), (2, 2), (4, 2), (6, 2)]
+        x_rows = [keep.tile([P, 2, D], BF16, align_bytes=64, name="x_rows%d" % n) for n in range(4)]
+        x_turned = {}
+        x_grouped = {}
+
+        words = W_ih0_words[0].rearrange("p (g n) -> p g n", g=4)
+        scales = W_ih0_scales[0].rearrange("q (g n) -> q g n", g=4)
+
+        def load_x(queue, n):
+            queue.dma_start(out=x_rows[n][:], in_=x[2 * n * P:2 * (n + 1) * P, :].rearrange("(b p) k -> p b k", p=P))
+
+        def turn_x(c):
+            b0, n = chunks[c]
+            bank = turn_psum.tile([P, BANK], F32, tag="turn", name="x_bank")
+            view = bank[:, 0:n * 2 * P].rearrange("p (b u r) -> p b u r", b=n, u=2)
+            for b in range(n):
+                pairs = x_rows[(b0 + b) // 2][:, (b0 + b) % 2, :].bitcast(F32)
+                for u in range(2):
+                    nc.tensor.transpose(view[:, b, u, :], pairs[:, u:2 * P:2], ident[:])
+            x_turned[c] = view
+
+        def group_x(c):
+            n = chunks[c][1]
+            grouped = keep.tile([P, n * 4 * P], BF16, align_bytes=64, name="x_grouped%d" % c)
+            nc.vector.tensor_copy(
+                out=grouped[:].bitcast(F32).rearrange("p (b r u) -> p b r u", b=n, u=2),
+                in_=x_turned[c].rearrange("p b u r -> p b r u"),
+            )
+            x_grouped[c] = grouped
+
+        def quantize_x(c):
+            b0, n = chunks[c]
+            cols = slice(b0 * P, (b0 + n) * P)
+            nc.vector.quantize_mx(out=x_codes[:, cols].bitcast(E5M2X4), scales=x_scales[:, cols], in_=x_grouped[c][:])
+
+        def sum_bias(gates, dest):
+            bank = turn_psum.tile([P, BANK], F32, tag="turn", name="bias_bank")
+            for n, g in enumerate(gates):
+                nc.tensor.matmul(bank[:, n * TILES:(n + 1) * TILES], lhsT=bias_rows[:, g, :], rhs=pick[:], start=True, stop=True)
+            nc.vector.tensor_copy(out=dest[:].rearrange("p g j -> p (g j)"), in_=bank[:, 0:len(gates) * TILES])
+
+        pre = {}
+
+        def multiply(gate, s):
+            j, t0, n = units[s]
+            if gate == GATE_O:
+                codes, plane = w_o[:, 2 * P * j:2 * P * (j + 1)], ws_o[:, P * j:P * (j + 1)]
+            else:
+                plane = ws_ig[:, gate, P * j:P * (j + 1)]
+                if j < EARLY:
+                    codes = w_ig_early[:, gate, 2 * P * j:2 * P * (j + 1)]
+                else:
+                    codes = w_ig_late[:, gate, 2 * P * (j - EARLY):2 * P * (j - EARLY + 1)]
+            bank = gate_psum.tile([P, BANK], F32, tag="gate", name="gate_bank")
+            done = 0
+            for width in (P, 2 * P, 4 * P):
+                if n & width:
+                    cols = slice(t0 + done, t0 + done + width)
+                    nc.tensor.matmul_mx(
+                        out=bank[:, done:done + width],
+                        lhsT=codes.bitcast(E2M1X4), lhsT_scale=plane,
+                        rhs=x_codes[:, cols].bitcast(E5M2X4), rhs_scale=x_scales[:, cols],
+                        start=True, stop=True,
+                    )
+                    done += width
+            pre[gate, s] = bank
+
+        def activate(gate, s):
+            j, t0, n = units[s]
+            bias = bias_o[:, 0, j:j + 1] if gate == GATE_O else bias_ig[:, gate, j:j + 1]
+            value = work.tile([P, BANK], F32, tag="gate%d" % gate, name="value")
+            nc.scalar.activation(out=value[:, 0:n], in_=pre[gate, s][:, 0:n],
+                                 func=ACT.Tanh if gate == GATE_G else ACT.Sigmoid, bias=bias)
+            return value
+
+        def turn(src, n):
+            bank = turn_psum.tile([P, BANK], F32, tag="turn", name="turn_bank")
+            for b in range(n // P):
+                nc.tensor.transpose(bank[:, b * P:(b + 1) * P], src[:, b * P:(b + 1) * P], ident[:])
+            return bank
+
+        def finish(s, cell_t, sig_o_t):
+            j, t0, n = units[s]
+            step = n // 2 if s == last else n
+            for a in range(0, n, step):
+                tanh_c = work.tile([P, BANK], F32, tag="tanh_c", name="tanh_c")
+                nc.scalar.activation(out=tanh_c[:, 0:step], in_=cell_t[:, a:a + step], func=ACT.Tanh)
+                result = work.tile([P, BANK], F32, tag="result", name="result", bufs=4)
+                nc.vector.tensor_tensor(out=result[:, 0:step], in0=sig_o_t[:, a:a + step], in1=tanh_c[:, 0:step], op=ALU.mult)
+                nc.sync.dma_start(
+                    out=out[t0 + a:t0 + a + step, j * P:(j + 1) * P].rearrange("(b p) c -> p b c", p=P),
+                    in_=result[:, 0:step].rearrange("p (b c) -> p b c", c=P),
+                )
+
+        def load_bias(queue, n, gates, slots):
+            rows = (b_ih0, b_hh0)[n].rearrange("(g j c) -> j g c", g=4, c=P)
+            queue.dma_start(out=bias_rows[n * TILES:(n + 1) * TILES, slots, :], in_=rows[:, gates, :])
+
+        nc.vector.memset(ident[:], 0.0)
+        nc.vector.memset(bias_rows[:], 0.0)
+        make_identity(nc, ident[:], nomemset=True)
+
+        load_x(nc.sync, 0)
+        for r in range(4):
+            nc.sync.dma_start(out=ws_ig[r:P:32, :, :].bitcast(I32), in_=scales[r:16:4, 0:3:2, :].bitcast(I32))
+        nc.sync.dma_start(out=w_ig_early[:].bitcast(I32), in_=words[:, 0:3:2, 0:2 * P * EARLY].bitcast(I32))
+        for n in range(2):
+            load_bias(nc.sync, n, slice(0, 3, 2), slice(0, 2))
+        load_x(nc.gpsimd, 1)
+        for n in range(2):
+            load_bias(nc.gpsimd, n, slice(3, 4), slice(2, 3))
+        for r in range(4):
+            nc.sync.dma_start(out=ws_o[r:P:32, :].bitcast(I32), in_=scales[r:16:4, 3, :].bitcast(I32))
+        nc.sync.dma_start(out=w_o[:].bitcast(I32), in_=words[:, 3, :].bitcast(I32))
+        nc.sync.dma_start(out=w_ig_late[:].bitcast(I32), in_=words[:, 0:3:2, 2 * P * EARLY:2 * H].bitcast(I32))
+        load_x(nc.sync, 2)
+        load_x(nc.sync, 3)
+
+        nc.vector.tensor_tensor(out=pick[:], in0=ident[:, 0:TILES], in1=ident[:, TILES:2 * TILES], op=ALU.add)
+
+        turn_x(0)
+        group_x(0)
+        quantize_x(0)
+        turn_x(1)
+        sum_bias((GATE_I, GATE_G), bias_ig)
+        multiply(GATE_I, 0)
+        multiply(GATE_G, 0)
+        group_x(1)
+        quantize_x(1)
+
+        cell_t = {}
+        for s in range(last + 2):
+            if s <= last:
+                n = units[s][2]
+                sig_i = activate(GATE_I, s)
+                if s < last:
+                    multiply(GATE_I, s + 1)
+                    multiply(GATE_G, s + 1)
+                tanh_g = activate(GATE_G, s)
+                if s == 0:
+                    turn_x(2)
+                cell = work.tile([P, BANK], F32, tag="cell", name="cell")
+                nc.vector.tensor_tensor(out=cell[:, 0:n], in0=sig_i[:, 0:n], in1=tanh_g[:, 0:n], op=ALU.mult)
+                if s == 0:
+                    group_x(2)
+                    quantize_x(2)
+                    sum_bias((GATE_O,), bias_o)
+                if s in (5, 6):
+                    quantize_x(s - 2)
+                multiply(GATE_O, s)
+            if s > 0:
+                sig_o = activate(GATE_O, s - 1)
+                sig_o_t = turn(sig_o, units[s - 1][2])
+            if s <= last:
+                cell_t[s] = turn(cell, n)
+            if s in (4, 5):
+                turn_x(s - 1)
+            if s > 0:
+                finish(s - 1, cell_t[s - 1], sig_o_t)
+            if s in (4, 5):
+                group_x(s - 1)

@@ -1,3 +1,4 @@
+import math
 from contextlib import ExitStack
 
 import concourse.mybir as mybir
@@ -22,20 +23,43 @@ BANK = 512
 TILES = H // P
 GATE_I, GATE_G, GATE_O = 0, 1, 2
 EARLY = 2
+LAG = 2
+EARLY_W = 4
+X_STEP = 2
+LAST_PIECE = 256
+POLY_UNITS = (3, 7, 10)
+POLY_DEGREE = 8
+POLY_PACE = (6, 5, 5, 2)
+
+
+def tanh_over_c_in_c_squared(degree):
+    count = degree + 1
+    nodes = [0.5 - 0.5 * math.cos(math.pi * (k + 0.5) / count) for k in range(count)]
+    diffs = [math.tanh(math.sqrt(u)) / math.sqrt(u) for u in nodes]
+    for order in range(1, count):
+        for k in range(degree, order - 1, -1):
+            diffs[k] = (diffs[k] - diffs[k - 1]) / (nodes[k] - nodes[k - order])
+    coeffs = [diffs[degree]]
+    for k in range(degree - 1, -1, -1):
+        coeffs = [low - nodes[k] * high for low, high in zip([0.0] + coeffs, coeffs + [0.0])]
+        coeffs[0] += diffs[k]
+    return coeffs
 
 
 def tile_lstmbaseline_pa_kernel(tc, x, W_ih0_words, W_ih0_scales, b_ih0, b_hh0, out):
     nc = tc.nc
 
-    units = [(0, 0, P), (1, 0, 2 * P), (0, P, 3 * P), (1, 2 * P, 2 * P)]
-    units += [(j, 0, BANK) for j in range(EARLY, TILES)] + [(j, BANK, BANK) for j in range(TILES)]
+    units = [(j, t0, BANK) for t0 in (0, BANK) for j in range(TILES)]
+    coeffs = tanh_over_c_in_c_squared(POLY_DEGREE)
     last = len(units) - 1
 
     with ExitStack() as ctx:
         keep = ctx.enter_context(tc.tile_pool(name="keep", bufs=1))
         work = ctx.enter_context(tc.tile_pool(name="work", bufs=3))
         gate_psum = ctx.enter_context(tc.psum_pool(name="gate_psum", bufs=4))
-        turn_psum = ctx.enter_context(tc.psum_pool(name="turn_psum", bufs=4))
+        cell_psum = ctx.enter_context(tc.psum_pool(name="cell_psum", bufs=1))
+        factor_psum = ctx.enter_context(tc.psum_pool(name="factor_psum", bufs=1))
+        spare_psum = ctx.enter_context(tc.psum_pool(name="spare_psum", bufs=2))
         ctx.enter_context(tc.manual_schedule())
 
         ident = keep.tile([P, P], F32, align_bytes=64)
@@ -43,15 +67,15 @@ def tile_lstmbaseline_pa_kernel(tc, x, W_ih0_words, W_ih0_scales, b_ih0, b_hh0, 
         bias_rows = keep.tile([P, 3, P], BF16, align_bytes=64)
         bias_ig = keep.tile([P, 2, TILES], F32, align_bytes=64)
         bias_o = keep.tile([P, 1, TILES], F32, align_bytes=64)
-        w_ig_early = keep.tile([P, 2, 2 * P * EARLY], U8, align_bytes=64)
-        w_ig_late = keep.tile([P, 2, 2 * P * (TILES - EARLY)], U8, align_bytes=64)
+        w_ig_early = keep.tile([P, 2, 2 * P * EARLY_W], U8, align_bytes=64)
+        w_ig_late = keep.tile([P, 2, 2 * P * (TILES - EARLY_W)], U8, align_bytes=64)
         w_o = keep.tile([P, 2 * H], U8, align_bytes=64)
         ws_ig = keep.tile([P, 2, H], U8, align_bytes=64)
         ws_o = keep.tile([P, H], U8, align_bytes=64)
         x_codes = keep.tile([P, B], U32, align_bytes=64)
         x_scales = keep.tile([P, B], U8, align_bytes=64)
 
-        chunks = [(0, 1), (1, 1), (2, 2), (4, 2), (6, 2)]
+        chunks = [(0, 1), (1, 1), (2, 1), (3, 1), (4, 2), (6, 2)]
         x_rows = [keep.tile([P, 2, D], BF16, align_bytes=64, name="x_rows%d" % n) for n in range(4)]
         x_turned = {}
         x_grouped = {}
@@ -62,9 +86,9 @@ def tile_lstmbaseline_pa_kernel(tc, x, W_ih0_words, W_ih0_scales, b_ih0, b_hh0, 
         def load_x(queue, n):
             queue.dma_start(out=x_rows[n][:], in_=x[2 * n * P:2 * (n + 1) * P, :].rearrange("(b p) k -> p b k", p=P))
 
-        def turn_x(c):
+        def turn_x(c, pool):
             b0, n = chunks[c]
-            bank = turn_psum.tile([P, BANK], F32, tag="turn", name="x_bank")
+            bank = pool.tile([P, BANK], F32, name="bank")
             view = bank[:, 0:n * 2 * P].rearrange("p (b u r) -> p b u r", b=n, u=2)
             for b in range(n):
                 pairs = x_rows[(b0 + b) // 2][:, (b0 + b) % 2, :].bitcast(F32)
@@ -72,10 +96,10 @@ def tile_lstmbaseline_pa_kernel(tc, x, W_ih0_words, W_ih0_scales, b_ih0, b_hh0, 
                     nc.tensor.transpose(view[:, b, u, :], pairs[:, u:2 * P:2], ident[:])
             x_turned[c] = view
 
-        def group_x(c):
+        def group_x(c, copy):
             n = chunks[c][1]
             grouped = keep.tile([P, n * 4 * P], BF16, align_bytes=64, name="x_grouped%d" % c)
-            nc.vector.tensor_copy(
+            copy(
                 out=grouped[:].bitcast(F32).rearrange("p (b r u) -> p b r u", b=n, u=2),
                 in_=x_turned[c].rearrange("p b u r -> p b r u"),
             )
@@ -86,129 +110,221 @@ def tile_lstmbaseline_pa_kernel(tc, x, W_ih0_words, W_ih0_scales, b_ih0, b_hh0, 
             cols = slice(b0 * P, (b0 + n) * P)
             nc.vector.quantize_mx(out=x_codes[:, cols].bitcast(E5M2X4), scales=x_scales[:, cols], in_=x_grouped[c][:])
 
-        def sum_bias(gates, dest):
-            bank = turn_psum.tile([P, BANK], F32, tag="turn", name="bias_bank")
+        def sum_bias(gates, dest, copy):
+            bank = factor_psum.tile([P, BANK], F32, name="bank")
             for n, g in enumerate(gates):
                 nc.tensor.matmul(bank[:, n * TILES:(n + 1) * TILES], lhsT=bias_rows[:, g, :], rhs=pick[:], start=True, stop=True)
-            nc.vector.tensor_copy(out=dest[:].rearrange("p g j -> p (g j)"), in_=bank[:, 0:len(gates) * TILES])
+            copy(out=dest[:].rearrange("p g j -> p (g j)"), in_=bank[:, 0:len(gates) * TILES])
 
         pre = {}
 
-        def multiply(gate, s):
+        def multiply(gate, s, tokens=slice(0, BANK)):
             j, t0, n = units[s]
             if gate == GATE_O:
                 codes, plane = w_o[:, 2 * P * j:2 * P * (j + 1)], ws_o[:, P * j:P * (j + 1)]
             else:
                 plane = ws_ig[:, gate, P * j:P * (j + 1)]
-                if j < EARLY:
+                if j < EARLY_W:
                     codes = w_ig_early[:, gate, 2 * P * j:2 * P * (j + 1)]
                 else:
-                    codes = w_ig_late[:, gate, 2 * P * (j - EARLY):2 * P * (j - EARLY + 1)]
-            bank = gate_psum.tile([P, BANK], F32, tag="gate", name="gate_bank")
-            done = 0
-            for width in (P, 2 * P, 4 * P):
-                if n & width:
-                    cols = slice(t0 + done, t0 + done + width)
-                    nc.tensor.matmul_mx(
-                        out=bank[:, done:done + width],
-                        lhsT=codes.bitcast(E2M1X4), lhsT_scale=plane,
-                        rhs=x_codes[:, cols].bitcast(E5M2X4), rhs_scale=x_scales[:, cols],
-                        start=True, stop=True,
-                    )
-                    done += width
-            pre[gate, s] = bank
+                    codes = w_ig_late[:, gate, 2 * P * (j - EARLY_W):2 * P * (j - EARLY_W + 1)]
+            if tokens.start == 0:
+                bank = gate_psum.tile([P, BANK], F32, name="bank")
+                pre[gate, s] = bank[:, :]
+            done = tokens.start
+            for width in [w for w in (P, 2 * P, BANK) if (tokens.stop - tokens.start) & w]:
+                cols = slice(t0 + done, t0 + done + width)
+                nc.tensor.matmul_mx(
+                    out=pre[gate, s][:, done:done + width],
+                    lhsT=codes.bitcast(E2M1X4), lhsT_scale=plane,
+                    rhs=x_codes[:, cols].bitcast(E5M2X4), rhs_scale=x_scales[:, cols],
+                    start=True, stop=True,
+                )
+                done += width
 
-        def activate(gate, s):
+        def fresh(tag, n, bufs):
+            tile = work.tile([P, BANK], F32, tag=tag, name=tag, bufs=bufs)
+            return tile[:, 0:n]
+
+        value = {}
+
+        def activate(gate, s, cols=None):
             j, t0, n = units[s]
+            cols = cols or slice(0, n)
             bias = bias_o[:, 0, j:j + 1] if gate == GATE_O else bias_ig[:, gate, j:j + 1]
-            value = work.tile([P, BANK], F32, tag="gate%d" % gate, name="value")
-            nc.scalar.activation(out=value[:, 0:n], in_=pre[gate, s][:, 0:n],
+            if cols.start == 0:
+                value[gate, s] = fresh("gate%d" % gate, n, 4)
+            nc.scalar.activation(out=value[gate, s][:, cols], in_=pre[gate, s][:, cols],
                                  func=ACT.Tanh if gate == GATE_G else ACT.Sigmoid, bias=bias)
-            return value
 
-        def turn(src, n):
-            bank = turn_psum.tile([P, BANK], F32, tag="turn", name="turn_bank")
+        def product(engine, tag, a, b):
+            result = fresh(tag, a.shape[1], 4)
+            engine.tensor_tensor(out=result, in0=a, in1=b, op=ALU.mult)
+            return result
+
+        def turn(pool, src):
+            n = src.shape[1]
+            bank = pool.tile([P, BANK], F32, name="bank")
             for b in range(n // P):
                 nc.tensor.transpose(bank[:, b * P:(b + 1) * P], src[:, b * P:(b + 1) * P], ident[:])
-            return bank
+            return bank[:, 0:n]
 
-        def finish(s, cell_t, sig_o_t):
+        def store(s, cols, result):
             j, t0, n = units[s]
-            step = n // 2 if s == last else n
-            for a in range(0, n, step):
-                tanh_c = work.tile([P, BANK], F32, tag="tanh_c", name="tanh_c")
-                nc.scalar.activation(out=tanh_c[:, 0:step], in_=cell_t[:, a:a + step], func=ACT.Tanh)
-                result = work.tile([P, BANK], F32, tag="result", name="result", bufs=4)
-                nc.vector.tensor_tensor(out=result[:, 0:step], in0=sig_o_t[:, a:a + step], in1=tanh_c[:, 0:step], op=ALU.mult)
-                nc.sync.dma_start(
-                    out=out[t0 + a:t0 + a + step, j * P:(j + 1) * P].rearrange("(b p) c -> p b c", p=P),
-                    in_=result[:, 0:step].rearrange("p (b c) -> p b c", c=P),
-                )
+            nc.sync.dma_start(
+                out=out[t0 + cols.start:t0 + cols.stop, j * P:(j + 1) * P].rearrange("(b p) c -> p b c", p=P),
+                in_=result.rearrange("p (b c) -> p b c", c=P),
+            )
+
+        tanh_c = {}
+
+        def squash(s, cols):
+            tanh_c[s, cols.start] = fresh("tanh_c", cols.stop - cols.start, 4)
+            nc.scalar.activation(out=tanh_c[s, cols.start], in_=cell_t[s][:, cols], func=ACT.Tanh)
+
+        def finish(s, cols, factor_cols):
+            result = fresh("result", cols.stop - cols.start, 8)
+            nc.vector.tensor_tensor(out=result, in0=factor_cols, in1=tanh_c[s, cols.start], op=ALU.mult)
+            store(s, cols, result)
+
+        horner = {}
+
+        def horner_step(s, index):
+            half, k = index % 2, index // 2
+            cols = slice(half * BANK // 2, (half + 1) * BANK // 2)
+            u = cell_t[s][:, cols]
+            if k == 0:
+                nxt = fresh("horner", BANK // 2, 4)
+                nc.vector.tensor_scalar(out=nxt, in0=u, scalar1=coeffs[POLY_DEGREE], scalar2=coeffs[POLY_DEGREE - 1],
+                                        op0=ALU.mult, op1=ALU.add)
+            elif k == 1:
+                nxt = fresh("horner", BANK // 2, 4)
+                nc.vector.tensor_tensor(out=nxt, in0=u, in1=horner[half], op=ALU.mult)
+            elif k < POLY_DEGREE:
+                nxt = fresh("horner", BANK // 2, 4)
+                nc.vector.scalar_tensor_tensor(out=nxt, in0=horner[half], scalar=coeffs[POLY_DEGREE - k], in1=u,
+                                               op0=ALU.add, op1=ALU.mult)
+            else:
+                nxt = fresh("result", BANK // 2, 8)
+                nc.vector.scalar_tensor_tensor(out=nxt, in0=horner[half], scalar=coeffs[0], in1=factor_t[s][:, cols],
+                                               op0=ALU.add, op1=ALU.mult)
+                store(s, cols, nxt)
+            horner[half] = nxt
 
         def load_bias(queue, n, gates, slots):
             rows = (b_ih0, b_hh0)[n].rearrange("(g j c) -> j g c", g=4, c=P)
             queue.dma_start(out=bias_rows[n * TILES:(n + 1) * TILES, slots, :], in_=rows[:, gates, :])
 
-        nc.vector.memset(ident[:], 0.0)
         nc.vector.memset(bias_rows[:], 0.0)
-        make_identity(nc, ident[:], nomemset=True)
+        nc.vector.memset(ident[:], 0.0)
 
         load_x(nc.sync, 0)
-        for r in range(4):
-            nc.sync.dma_start(out=ws_ig[r:P:32, :, :].bitcast(I32), in_=scales[r:16:4, 0:3:2, :].bitcast(I32))
-        nc.sync.dma_start(out=w_ig_early[:].bitcast(I32), in_=words[:, 0:3:2, 0:2 * P * EARLY].bitcast(I32))
+        load_x(nc.sync, 1)
+        nc.gpsimd.dma_start(out=w_ig_early[:].bitcast(I32), in_=words[:, 0:3:2, 0:2 * P * EARLY_W].bitcast(I32))
+        make_identity(nc, ident[:], nomemset=True)
         for n in range(2):
             load_bias(nc.sync, n, slice(0, 3, 2), slice(0, 2))
-        load_x(nc.gpsimd, 1)
+        for r in range(4):
+            nc.sync.dma_start(out=ws_ig[r:P:32, :, :].bitcast(I32), in_=scales[r:16:4, 0:3:2, :].bitcast(I32))
         for n in range(2):
             load_bias(nc.gpsimd, n, slice(3, 4), slice(2, 3))
+        nc.sync.dma_start(out=w_o[:].bitcast(I32), in_=words[:, 3, :].bitcast(I32))
         for r in range(4):
             nc.sync.dma_start(out=ws_o[r:P:32, :].bitcast(I32), in_=scales[r:16:4, 3, :].bitcast(I32))
-        nc.sync.dma_start(out=w_o[:].bitcast(I32), in_=words[:, 3, :].bitcast(I32))
-        nc.sync.dma_start(out=w_ig_late[:].bitcast(I32), in_=words[:, 0:3:2, 2 * P * EARLY:2 * H].bitcast(I32))
+        nc.sync.dma_start(out=w_ig_late[:].bitcast(I32), in_=words[:, 0:3:2, 2 * P * EARLY_W:2 * H].bitcast(I32))
         load_x(nc.sync, 2)
         load_x(nc.sync, 3)
 
         nc.vector.tensor_tensor(out=pick[:], in0=ident[:, 0:TILES], in1=ident[:, TILES:2 * TILES], op=ALU.add)
 
-        turn_x(0)
-        group_x(0)
+        turn_x(0, spare_psum)
+        turn_x(1, spare_psum)
+        group_x(0, nc.vector.tensor_copy)
+        group_x(1, nc.vector.tensor_copy)
         quantize_x(0)
-        turn_x(1)
-        sum_bias((GATE_I, GATE_G), bias_ig)
-        multiply(GATE_I, 0)
-        multiply(GATE_G, 0)
-        group_x(1)
+        turn_x(2, cell_psum)
         quantize_x(1)
+        sum_bias((GATE_I, GATE_G), bias_ig, nc.vector.tensor_copy)
+        group_x(2, nc.vector.tensor_copy)
+        turn_x(3, spare_psum)
+        group_x(3, nc.vector.tensor_copy)
+        quantize_x(2)
+        quantize_x(3)
 
-        cell_t = {}
-        for s in range(last + 2):
-            if s <= last:
-                n = units[s][2]
-                sig_i = activate(GATE_I, s)
-                if s < last:
-                    multiply(GATE_I, s + 1)
-                    multiply(GATE_G, s + 1)
-                tanh_g = activate(GATE_G, s)
-                if s == 0:
-                    turn_x(2)
-                cell = work.tile([P, BANK], F32, tag="cell", name="cell")
-                nc.vector.tensor_tensor(out=cell[:, 0:n], in0=sig_i[:, 0:n], in1=tanh_g[:, 0:n], op=ALU.mult)
-                if s == 0:
-                    group_x(2)
-                    quantize_x(2)
-                    sum_bias((GATE_O,), bias_o)
-                if s in (5, 6):
-                    quantize_x(s - 2)
-                multiply(GATE_O, s)
-            if s > 0:
-                sig_o = activate(GATE_O, s - 1)
-                sig_o_t = turn(sig_o, units[s - 1][2])
-            if s <= last:
-                cell_t[s] = turn(cell, n)
-            if s in (4, 5):
-                turn_x(s - 1)
-            if s > 0:
-                finish(s - 1, cell_t[s - 1], sig_o_t)
-            if s in (4, 5):
-                group_x(s - 1)
+        cell, square, factor, cell_t, factor_t = {}, {}, {}, {}, {}
+        first = (P, 2 * P)
+        for s in range(EARLY):
+            for gate in (GATE_I, GATE_G):
+                multiply(gate, s, slice(0, first[s]))
+        for s in range(EARLY):
+            for gate in (GATE_I, GATE_G):
+                activate(gate, s, slice(0, first[s]))
+        for s in range(EARLY):
+            for gate in (GATE_I, GATE_G):
+                multiply(gate, s, slice(first[s], BANK))
+        sum_bias((GATE_O,), bias_o, nc.vector.tensor_copy)
+        activate(GATE_I, 0, slice(first[0], BANK))
+        multiply(GATE_O, 0)
+        activate(GATE_G, 0, slice(first[0], BANK))
+        multiply(GATE_I, 2)
+        cell[0] = product(nc.gpsimd, "cell", value[GATE_I, 0], value[GATE_G, 0])
+        activate(GATE_I, 1, slice(first[1], BANK))
+        multiply(GATE_G, 2)
+        activate(GATE_G, 1, slice(first[1], BANK))
+        multiply(GATE_O, 1)
+        cell[1] = product(nc.gpsimd, "cell", value[GATE_I, 1], value[GATE_G, 1])
+        activate(GATE_O, 0)
+        cell_t[0] = turn(cell_psum, cell[0])
+
+        def whole(s):
+            return slice(0, units[s][2])
+
+        for s in range(EARLY, last + 1):
+            activate(GATE_I, s)
+            if s < last:
+                multiply(GATE_I, s + 1)
+                multiply(GATE_G, s + 1)
+            activate(GATE_G, s)
+            cell[s] = product(nc.vector if s >= last - 0 else nc.gpsimd, "cell", value[GATE_I, s], value[GATE_G, s])
+            if s in POLY_UNITS:
+                square[s] = product(nc.gpsimd, "square", cell[s], cell[s])
+            multiply(GATE_O, s)
+            if s in (X_STEP + 1, X_STEP + 2):
+                quantize_x(s - X_STEP + 3)
+            if s in (X_STEP, X_STEP + 1):
+                turn_x(s - X_STEP + 4, spare_psum)
+                group_x(s - X_STEP + 4, nc.vector.tensor_copy)
+            if s - LAG - 1 in POLY_UNITS:
+                factor_t[s - LAG - 1] = turn(spare_psum, factor[s - LAG - 1])
+            for p in POLY_UNITS:
+                age = s - p - LAG
+                if 0 <= age < len(POLY_PACE):
+                    for index in range(sum(POLY_PACE[:age]), sum(POLY_PACE[:age + 1])):
+                        horner_step(p, index)
+            if s >= 1:
+                activate(GATE_O, s - 1)
+                if s - 1 in POLY_UNITS:
+                    factor[s - 1] = product(nc.gpsimd, "factor", value[GATE_O, s - 1], cell[s - 1])
+            if s == last:
+                cell_t[s - 1] = turn(spare_psum, cell[s - 1])
+            if s >= LAG and s - LAG not in POLY_UNITS:
+                factor_t[s - LAG] = turn(factor_psum, value[GATE_O, s - LAG])
+                squash(s - LAG, whole(s - LAG))
+                finish(s - LAG, whole(s - LAG), factor_t[s - LAG])
+            if s - 1 in POLY_UNITS:
+                cell_t[s - 1] = turn(spare_psum, square[s - 1])
+            elif 1 <= s < last:
+                cell_t[s - 1] = turn(cell_psum, cell[s - 1])
+
+        factor_t[last - 1] = turn(gate_psum, value[GATE_O, last - 1])
+        cell_t[last] = turn(spare_psum, cell[last])
+        squash(last - 1, whole(last - 1))
+        finish(last - 1, whole(last - 1), factor_t[last - 1])
+        pieces = [slice(0, BANK - LAST_PIECE), slice(BANK - LAST_PIECE, BANK)]
+        turned = []
+        for cols, pool in zip(pieces, (gate_psum, gate_psum)):
+            activate(GATE_O, last, cols)
+            turned.append(turn(pool, value[GATE_O, last][:, cols]))
+        for cols, factor_cols in zip(pieces, turned):
+            squash(last, cols)
+            finish(last, cols, factor_cols)

@@ -20,19 +20,26 @@ ALU = mybir.AluOpType
 
 P = 128
 BANK = 512
+HALF = BANK // 2
 TILES = H // P
+WORD_BYTES = 2
 GATE_I, GATE_G, GATE_O = 0, 1, 2
-EARLY = 2
-LAG = 2
-EARLY_W = 4
-X_STEP = 2
-LAST_PIECE = 256
-POLY_UNITS = (3, 7, 10)
+I_AND_G = slice(0, 3, 2)
+O_ONLY = slice(3, 4)
+
+EARLY_TILES = 3
+RAMP_UNITS = 2
+X_CHUNKS = ((0, 1), (1, 1), (2, 1), (3, 1), (4, 2), (6, 2))
+X_LATE_STEP = 2
+
 POLY_DEGREE = 8
+POLY_UNITS = (3, 7, 10)
 POLY_PACE = (6, 5, 5, 2)
+GATE_BUFS = 4
+RESULT_BUFS = 8
 
 
-def tanh_over_c_in_c_squared(degree):
+def tanh_over_c_coefficients(degree):
     count = degree + 1
     nodes = [0.5 - 0.5 * math.cos(math.pi * (k + 0.5) / count) for k in range(count)]
     diffs = [math.tanh(math.sqrt(u)) / math.sqrt(u) for u in nodes]
@@ -48,14 +55,15 @@ def tanh_over_c_in_c_squared(degree):
 
 def tile_lstmbaseline_pa_kernel(tc, x, W_ih0_words, W_ih0_scales, b_ih0, b_hh0, out):
     nc = tc.nc
-
-    units = [(j, t0, BANK) for t0 in (0, BANK) for j in range(TILES)]
-    coeffs = tanh_over_c_in_c_squared(POLY_DEGREE)
+    units = [(j, t0) for t0 in (0, BANK) for j in range(TILES)]
     last = len(units) - 1
+    whole = slice(0, BANK)
+    halves = (slice(0, HALF), slice(HALF, BANK))
+    coeffs = tanh_over_c_coefficients(POLY_DEGREE)
 
     with ExitStack() as ctx:
         keep = ctx.enter_context(tc.tile_pool(name="keep", bufs=1))
-        work = ctx.enter_context(tc.tile_pool(name="work", bufs=3))
+        work = ctx.enter_context(tc.tile_pool(name="work", bufs=GATE_BUFS))
         gate_psum = ctx.enter_context(tc.psum_pool(name="gate_psum", bufs=4))
         cell_psum = ctx.enter_context(tc.psum_pool(name="cell_psum", bufs=1))
         factor_psum = ctx.enter_context(tc.psum_pool(name="factor_psum", bufs=1))
@@ -67,264 +75,233 @@ def tile_lstmbaseline_pa_kernel(tc, x, W_ih0_words, W_ih0_scales, b_ih0, b_hh0, 
         bias_rows = keep.tile([P, 3, P], BF16, align_bytes=64)
         bias_ig = keep.tile([P, 2, TILES], F32, align_bytes=64)
         bias_o = keep.tile([P, 1, TILES], F32, align_bytes=64)
-        w_ig_early = keep.tile([P, 2, 2 * P * EARLY_W], U8, align_bytes=64)
-        w_ig_late = keep.tile([P, 2, 2 * P * (TILES - EARLY_W)], U8, align_bytes=64)
-        w_o = keep.tile([P, 2 * H], U8, align_bytes=64)
+        w_ig_early = keep.tile([P, 2, WORD_BYTES * P * EARLY_TILES], U8, align_bytes=64)
+        w_ig_late = keep.tile([P, 2, WORD_BYTES * P * (TILES - EARLY_TILES)], U8, align_bytes=64)
+        w_o = keep.tile([P, WORD_BYTES * H], U8, align_bytes=64)
         ws_ig = keep.tile([P, 2, H], U8, align_bytes=64)
         ws_o = keep.tile([P, H], U8, align_bytes=64)
         x_codes = keep.tile([P, B], U32, align_bytes=64)
         x_scales = keep.tile([P, B], U8, align_bytes=64)
-
-        chunks = [(0, 1), (1, 1), (2, 1), (3, 1), (4, 2), (6, 2)]
-        x_rows = [keep.tile([P, 2, D], BF16, align_bytes=64, name="x_rows%d" % n) for n in range(4)]
-        x_turned = {}
-        x_grouped = {}
+        x_rows = [keep.tile([P, 2, D], BF16, align_bytes=64, name="x_rows%d" % n) for n in range(B // (2 * P))]
 
         words = W_ih0_words[0].rearrange("p (g n) -> p g n", g=4)
         scales = W_ih0_scales[0].rearrange("q (g n) -> q g n", g=4)
 
-        def load_x(queue, n):
-            queue.dma_start(out=x_rows[n][:], in_=x[2 * n * P:2 * (n + 1) * P, :].rearrange("(b p) k -> p b k", p=P))
+        x_turned, x_grouped = {}, {}
 
-        def turn_x(c, pool):
-            b0, n = chunks[c]
+        def load_x(n):
+            nc.sync.dma_start(out=x_rows[n][:], in_=x[2 * n * P:2 * (n + 1) * P, :].rearrange("(b p) k -> p b k", p=P))
+
+        def turn_x(chunk, pool):
+            first_block, blocks = X_CHUNKS[chunk]
             bank = pool.tile([P, BANK], F32, name="bank")
-            view = bank[:, 0:n * 2 * P].rearrange("p (b u r) -> p b u r", b=n, u=2)
-            for b in range(n):
-                pairs = x_rows[(b0 + b) // 2][:, (b0 + b) % 2, :].bitcast(F32)
+            x_turned[chunk] = bank[:, 0:blocks * 2 * P].rearrange("p (b u r) -> p b u r", b=blocks, u=2)
+            for b in range(blocks):
+                n, slot = divmod(first_block + b, 2)
+                pairs = x_rows[n][:, slot, :].bitcast(F32)
                 for u in range(2):
-                    nc.tensor.transpose(view[:, b, u, :], pairs[:, u:2 * P:2], ident[:])
-            x_turned[c] = view
+                    nc.tensor.transpose(x_turned[chunk][:, b, u, :], pairs[:, u:2 * P:2], ident[:])
 
-        def group_x(c, copy):
-            n = chunks[c][1]
-            grouped = keep.tile([P, n * 4 * P], BF16, align_bytes=64, name="x_grouped%d" % c)
-            copy(
-                out=grouped[:].bitcast(F32).rearrange("p (b r u) -> p b r u", b=n, u=2),
-                in_=x_turned[c].rearrange("p b u r -> p b r u"),
+        def group_x(chunk):
+            blocks = X_CHUNKS[chunk][1]
+            x_grouped[chunk] = keep.tile([P, blocks * 4 * P], BF16, align_bytes=64, name="x_grouped%d" % chunk)
+            nc.vector.tensor_copy(
+                out=x_grouped[chunk][:].bitcast(F32).rearrange("p (b r u) -> p b r u", b=blocks, u=2),
+                in_=x_turned[chunk].rearrange("p b u r -> p b r u"),
             )
-            x_grouped[c] = grouped
 
-        def quantize_x(c):
-            b0, n = chunks[c]
-            cols = slice(b0 * P, (b0 + n) * P)
-            nc.vector.quantize_mx(out=x_codes[:, cols].bitcast(E5M2X4), scales=x_scales[:, cols], in_=x_grouped[c][:])
+        def quantize_x(chunk):
+            first_block, blocks = X_CHUNKS[chunk]
+            tokens = slice(first_block * P, (first_block + blocks) * P)
+            nc.vector.quantize_mx(out=x_codes[:, tokens].bitcast(E5M2X4), scales=x_scales[:, tokens], in_=x_grouped[chunk][:])
 
-        def sum_bias(gates, dest, copy):
+        def load_bias(queue, places, slots):
+            for n, vector in enumerate((b_ih0, b_hh0)):
+                rows = vector.rearrange("(g j c) -> j g c", g=4, c=P)
+                queue.dma_start(out=bias_rows[n * TILES:(n + 1) * TILES, slots, :], in_=rows[:, places, :])
+
+        def sum_bias(gates, dest):
             bank = factor_psum.tile([P, BANK], F32, name="bank")
-            for n, g in enumerate(gates):
-                nc.tensor.matmul(bank[:, n * TILES:(n + 1) * TILES], lhsT=bias_rows[:, g, :], rhs=pick[:], start=True, stop=True)
-            copy(out=dest[:].rearrange("p g j -> p (g j)"), in_=bank[:, 0:len(gates) * TILES])
+            for n, gate in enumerate(gates):
+                nc.tensor.matmul(bank[:, n * TILES:(n + 1) * TILES], lhsT=bias_rows[:, gate, :], rhs=pick[:], start=True, stop=True)
+            nc.vector.tensor_copy(out=dest[:].rearrange("p g j -> p (g j)"), in_=bank[:, 0:len(gates) * TILES])
 
-        pre = {}
+        sums, value = {}, {}
+        cell, square, factor = {}, {}, {}
+        cell_t, factor_t, tanh_c = {}, {}, {}
+        horner = {}
 
-        def multiply(gate, s, tokens=slice(0, BANK)):
-            j, t0, n = units[s]
-            if gate == GATE_O:
-                codes, plane = w_o[:, 2 * P * j:2 * P * (j + 1)], ws_o[:, P * j:P * (j + 1)]
-            else:
-                plane = ws_ig[:, gate, P * j:P * (j + 1)]
-                if j < EARLY_W:
-                    codes = w_ig_early[:, gate, 2 * P * j:2 * P * (j + 1)]
-                else:
-                    codes = w_ig_late[:, gate, 2 * P * (j - EARLY_W):2 * P * (j - EARLY_W + 1)]
-            if tokens.start == 0:
-                bank = gate_psum.tile([P, BANK], F32, name="bank")
-                pre[gate, s] = bank[:, :]
-            done = tokens.start
-            for width in [w for w in (P, 2 * P, BANK) if (tokens.stop - tokens.start) & w]:
-                cols = slice(t0 + done, t0 + done + width)
-                nc.tensor.matmul_mx(
-                    out=pre[gate, s][:, done:done + width],
-                    lhsT=codes.bitcast(E2M1X4), lhsT_scale=plane,
-                    rhs=x_codes[:, cols].bitcast(E5M2X4), rhs_scale=x_scales[:, cols],
-                    start=True, stop=True,
-                )
-                done += width
-
-        def fresh(tag, n, bufs):
+        def fresh(tag, width, bufs=GATE_BUFS):
             tile = work.tile([P, BANK], F32, tag=tag, name=tag, bufs=bufs)
-            return tile[:, 0:n]
+            return tile[:, 0:width]
 
-        value = {}
+        def multiply(gate, s, cols=whole):
+            j, t0 = units[s]
+            if gate == GATE_O:
+                codes, first_tile, plane = w_o[:, :], 0, ws_o[:, P * j:P * (j + 1)]
+            elif j < EARLY_TILES:
+                codes, first_tile, plane = w_ig_early[:, gate, :], 0, ws_ig[:, gate, P * j:P * (j + 1)]
+            else:
+                codes, first_tile, plane = w_ig_late[:, gate, :], EARLY_TILES, ws_ig[:, gate, P * j:P * (j + 1)]
+            codes = codes[:, WORD_BYTES * P * (j - first_tile):WORD_BYTES * P * (j - first_tile + 1)]
+            if cols.start == 0:
+                bank = gate_psum.tile([P, BANK], F32, name="bank")
+                sums[gate, s] = bank[:, :]
+            tokens = slice(t0 + cols.start, t0 + cols.stop)
+            nc.tensor.matmul_mx(
+                out=sums[gate, s][:, cols],
+                lhsT=codes.bitcast(E2M1X4), lhsT_scale=plane,
+                rhs=x_codes[:, tokens].bitcast(E5M2X4), rhs_scale=x_scales[:, tokens],
+                start=True, stop=True,
+            )
 
-        def activate(gate, s, cols=None):
-            j, t0, n = units[s]
-            cols = cols or slice(0, n)
+        def activate(gate, s, cols=whole):
+            j = units[s][0]
             bias = bias_o[:, 0, j:j + 1] if gate == GATE_O else bias_ig[:, gate, j:j + 1]
             if cols.start == 0:
-                value[gate, s] = fresh("gate%d" % gate, n, 4)
-            nc.scalar.activation(out=value[gate, s][:, cols], in_=pre[gate, s][:, cols],
+                value[gate, s] = fresh("gate%d" % gate, BANK)
+            nc.scalar.activation(out=value[gate, s][:, cols], in_=sums[gate, s][:, cols],
                                  func=ACT.Tanh if gate == GATE_G else ACT.Sigmoid, bias=bias)
 
         def product(engine, tag, a, b):
-            result = fresh(tag, a.shape[1], 4)
+            result = fresh(tag, BANK)
             engine.tensor_tensor(out=result, in0=a, in1=b, op=ALU.mult)
             return result
 
         def turn(pool, src):
-            n = src.shape[1]
+            width = src.shape[1]
             bank = pool.tile([P, BANK], F32, name="bank")
-            for b in range(n // P):
+            for b in range(width // P):
                 nc.tensor.transpose(bank[:, b * P:(b + 1) * P], src[:, b * P:(b + 1) * P], ident[:])
-            return bank[:, 0:n]
+            return bank[:, 0:width]
 
         def store(s, cols, result):
-            j, t0, n = units[s]
+            j, t0 = units[s]
             nc.sync.dma_start(
                 out=out[t0 + cols.start:t0 + cols.stop, j * P:(j + 1) * P].rearrange("(b p) c -> p b c", p=P),
                 in_=result.rearrange("p (b c) -> p b c", c=P),
             )
 
-        tanh_c = {}
-
-        def squash(s, cols):
-            tanh_c[s, cols.start] = fresh("tanh_c", cols.stop - cols.start, 4)
-            nc.scalar.activation(out=tanh_c[s, cols.start], in_=cell_t[s][:, cols], func=ACT.Tanh)
-
         def finish(s, cols, factor_cols):
-            result = fresh("result", cols.stop - cols.start, 8)
-            nc.vector.tensor_tensor(out=result, in0=factor_cols, in1=tanh_c[s, cols.start], op=ALU.mult)
+            width = cols.stop - cols.start
+            tanh_c[s] = fresh("tanh_c", width)
+            nc.scalar.activation(out=tanh_c[s], in_=cell_t[s][:, cols], func=ACT.Tanh)
+            result = fresh("result", width, RESULT_BUFS)
+            nc.vector.tensor_tensor(out=result, in0=factor_cols, in1=tanh_c[s], op=ALU.mult)
             store(s, cols, result)
 
-        horner = {}
-
         def horner_step(s, index):
-            half, k = index % 2, index // 2
-            cols = slice(half * BANK // 2, (half + 1) * BANK // 2)
-            u = cell_t[s][:, cols]
+            k, half = divmod(index, 2)
+            u = cell_t[s][:, halves[half]]
             if k == 0:
-                nxt = fresh("horner", BANK // 2, 4)
-                nc.vector.tensor_scalar(out=nxt, in0=u, scalar1=coeffs[POLY_DEGREE], scalar2=coeffs[POLY_DEGREE - 1],
+                acc = fresh("horner", HALF)
+                nc.vector.tensor_scalar(out=acc, in0=u, scalar1=coeffs[POLY_DEGREE], scalar2=coeffs[POLY_DEGREE - 1],
                                         op0=ALU.mult, op1=ALU.add)
             elif k == 1:
-                nxt = fresh("horner", BANK // 2, 4)
-                nc.vector.tensor_tensor(out=nxt, in0=u, in1=horner[half], op=ALU.mult)
+                acc = fresh("horner", HALF)
+                nc.vector.tensor_tensor(out=acc, in0=u, in1=horner[half], op=ALU.mult)
             elif k < POLY_DEGREE:
-                nxt = fresh("horner", BANK // 2, 4)
-                nc.vector.scalar_tensor_tensor(out=nxt, in0=horner[half], scalar=coeffs[POLY_DEGREE - k], in1=u,
+                acc = fresh("horner", HALF)
+                nc.vector.scalar_tensor_tensor(out=acc, in0=horner[half], scalar=coeffs[POLY_DEGREE - k], in1=u,
                                                op0=ALU.add, op1=ALU.mult)
             else:
-                nxt = fresh("result", BANK // 2, 8)
-                nc.vector.scalar_tensor_tensor(out=nxt, in0=horner[half], scalar=coeffs[0], in1=factor_t[s][:, cols],
+                acc = fresh("result", HALF, RESULT_BUFS)
+                nc.vector.scalar_tensor_tensor(out=acc, in0=horner[half], scalar=coeffs[0], in1=factor_t[s][:, halves[half]],
                                                op0=ALU.add, op1=ALU.mult)
-                store(s, cols, nxt)
-            horner[half] = nxt
-
-        def load_bias(queue, n, gates, slots):
-            rows = (b_ih0, b_hh0)[n].rearrange("(g j c) -> j g c", g=4, c=P)
-            queue.dma_start(out=bias_rows[n * TILES:(n + 1) * TILES, slots, :], in_=rows[:, gates, :])
+                store(s, halves[half], acc)
+            horner[half] = acc
 
         nc.vector.memset(bias_rows[:], 0.0)
         nc.vector.memset(ident[:], 0.0)
-
-        load_x(nc.sync, 0)
-        load_x(nc.sync, 1)
-        nc.gpsimd.dma_start(out=w_ig_early[:].bitcast(I32), in_=words[:, 0:3:2, 0:2 * P * EARLY_W].bitcast(I32))
+        early_bytes = WORD_BYTES * P * EARLY_TILES
+        load_x(0)
+        load_bias(nc.sync, I_AND_G, slice(GATE_I, GATE_O))
+        load_x(1)
+        for r in range(4):
+            nc.sync.dma_start(out=ws_ig[r:P:32, :, :].bitcast(I32), in_=scales[r:16:4, I_AND_G, :].bitcast(I32))
         make_identity(nc, ident[:], nomemset=True)
-        for n in range(2):
-            load_bias(nc.sync, n, slice(0, 3, 2), slice(0, 2))
+        nc.gpsimd.dma_start(out=w_ig_early[:].bitcast(I32), in_=words[:, I_AND_G, 0:early_bytes].bitcast(I32))
+        load_bias(nc.gpsimd, O_ONLY, slice(GATE_O, GATE_O + 1))
+        nc.sync.dma_start(out=w_o[:].bitcast(I32), in_=words[:, O_ONLY.start, :].bitcast(I32))
         for r in range(4):
-            nc.sync.dma_start(out=ws_ig[r:P:32, :, :].bitcast(I32), in_=scales[r:16:4, 0:3:2, :].bitcast(I32))
-        for n in range(2):
-            load_bias(nc.gpsimd, n, slice(3, 4), slice(2, 3))
-        nc.sync.dma_start(out=w_o[:].bitcast(I32), in_=words[:, 3, :].bitcast(I32))
-        for r in range(4):
-            nc.sync.dma_start(out=ws_o[r:P:32, :].bitcast(I32), in_=scales[r:16:4, 3, :].bitcast(I32))
-        nc.sync.dma_start(out=w_ig_late[:].bitcast(I32), in_=words[:, 0:3:2, 2 * P * EARLY_W:2 * H].bitcast(I32))
-        load_x(nc.sync, 2)
-        load_x(nc.sync, 3)
-
+            nc.sync.dma_start(out=ws_o[r:P:32, :].bitcast(I32), in_=scales[r:16:4, O_ONLY.start, :].bitcast(I32))
+        nc.sync.dma_start(out=w_ig_late[:].bitcast(I32), in_=words[:, I_AND_G, early_bytes:WORD_BYTES * H].bitcast(I32))
+        load_x(2)
+        load_x(3)
         nc.vector.tensor_tensor(out=pick[:], in0=ident[:, 0:TILES], in1=ident[:, TILES:2 * TILES], op=ALU.add)
 
         turn_x(0, spare_psum)
         turn_x(1, spare_psum)
-        group_x(0, nc.vector.tensor_copy)
-        group_x(1, nc.vector.tensor_copy)
+        group_x(0)
+        group_x(1)
         quantize_x(0)
         turn_x(2, cell_psum)
         quantize_x(1)
-        sum_bias((GATE_I, GATE_G), bias_ig, nc.vector.tensor_copy)
-        group_x(2, nc.vector.tensor_copy)
+        sum_bias((GATE_I, GATE_G), bias_ig)
+        group_x(2)
         turn_x(3, spare_psum)
-        group_x(3, nc.vector.tensor_copy)
+        group_x(3)
         quantize_x(2)
         quantize_x(3)
 
-        cell, square, factor, cell_t, factor_t = {}, {}, {}, {}, {}
-        first = (P, 2 * P)
-        for s in range(EARLY):
-            for gate in (GATE_I, GATE_G):
-                multiply(gate, s, slice(0, first[s]))
-        for s in range(EARLY):
-            for gate in (GATE_I, GATE_G):
-                activate(gate, s, slice(0, first[s]))
-        for s in range(EARLY):
-            for gate in (GATE_I, GATE_G):
-                multiply(gate, s, slice(first[s], BANK))
-        sum_bias((GATE_O,), bias_o, nc.vector.tensor_copy)
-        activate(GATE_I, 0, slice(first[0], BANK))
-        multiply(GATE_O, 0)
-        activate(GATE_G, 0, slice(first[0], BANK))
-        multiply(GATE_I, 2)
-        cell[0] = product(nc.gpsimd, "cell", value[GATE_I, 0], value[GATE_G, 0])
-        activate(GATE_I, 1, slice(first[1], BANK))
-        multiply(GATE_G, 2)
-        activate(GATE_G, 1, slice(first[1], BANK))
-        multiply(GATE_O, 1)
-        cell[1] = product(nc.gpsimd, "cell", value[GATE_I, 1], value[GATE_G, 1])
+        ramp = [(gate, s) for s in range(RAMP_UNITS) for gate in (GATE_I, GATE_G)]
+        for gate, s in ramp:
+            multiply(gate, s, halves[0])
+        for gate, s in ramp:
+            activate(gate, s, halves[0])
+        for gate, s in ramp:
+            multiply(gate, s, halves[1])
+        sum_bias((GATE_O,), bias_o)
+        for (gate, s), following in zip(ramp, ((GATE_O, 0), (GATE_I, 2), (GATE_G, 2), (GATE_O, 1))):
+            activate(gate, s, halves[1])
+            multiply(*following)
+            if gate == GATE_G:
+                cell[s] = product(nc.gpsimd, "cell", value[GATE_I, s], value[GATE_G, s])
         activate(GATE_O, 0)
         cell_t[0] = turn(cell_psum, cell[0])
 
-        def whole(s):
-            return slice(0, units[s][2])
-
-        for s in range(EARLY, last + 1):
+        for s in range(RAMP_UNITS, last + 1):
             activate(GATE_I, s)
             if s < last:
                 multiply(GATE_I, s + 1)
                 multiply(GATE_G, s + 1)
             activate(GATE_G, s)
-            cell[s] = product(nc.vector if s >= last - 0 else nc.gpsimd, "cell", value[GATE_I, s], value[GATE_G, s])
+            cell[s] = product(nc.vector if s == last else nc.gpsimd, "cell", value[GATE_I, s], value[GATE_G, s])
             if s in POLY_UNITS:
                 square[s] = product(nc.gpsimd, "square", cell[s], cell[s])
             multiply(GATE_O, s)
-            if s in (X_STEP + 1, X_STEP + 2):
-                quantize_x(s - X_STEP + 3)
-            if s in (X_STEP, X_STEP + 1):
-                turn_x(s - X_STEP + 4, spare_psum)
-                group_x(s - X_STEP + 4, nc.vector.tensor_copy)
-            if s - LAG - 1 in POLY_UNITS:
-                factor_t[s - LAG - 1] = turn(spare_psum, factor[s - LAG - 1])
-            for p in POLY_UNITS:
-                age = s - p - LAG
+            late = s - X_LATE_STEP
+            if late in (1, 2):
+                quantize_x(3 + late)
+            if late in (0, 1):
+                turn_x(4 + late, spare_psum)
+                group_x(4 + late)
+            if s - 3 in POLY_UNITS:
+                factor_t[s - 3] = turn(spare_psum, factor[s - 3])
+            for poly in POLY_UNITS:
+                age = s - 2 - poly
                 if 0 <= age < len(POLY_PACE):
                     for index in range(sum(POLY_PACE[:age]), sum(POLY_PACE[:age + 1])):
-                        horner_step(p, index)
-            if s >= 1:
-                activate(GATE_O, s - 1)
-                if s - 1 in POLY_UNITS:
-                    factor[s - 1] = product(nc.gpsimd, "factor", value[GATE_O, s - 1], cell[s - 1])
+                        horner_step(poly, index)
+            activate(GATE_O, s - 1)
+            if s - 1 in POLY_UNITS:
+                factor[s - 1] = product(nc.gpsimd, "factor", value[GATE_O, s - 1], cell[s - 1])
             if s == last:
                 cell_t[s - 1] = turn(spare_psum, cell[s - 1])
-            if s >= LAG and s - LAG not in POLY_UNITS:
-                factor_t[s - LAG] = turn(factor_psum, value[GATE_O, s - LAG])
-                squash(s - LAG, whole(s - LAG))
-                finish(s - LAG, whole(s - LAG), factor_t[s - LAG])
+            if s - 2 not in POLY_UNITS:
+                factor_t[s - 2] = turn(factor_psum, value[GATE_O, s - 2])
+                finish(s - 2, whole, factor_t[s - 2])
             if s - 1 in POLY_UNITS:
                 cell_t[s - 1] = turn(spare_psum, square[s - 1])
-            elif 1 <= s < last:
+            elif s < last:
                 cell_t[s - 1] = turn(cell_psum, cell[s - 1])
 
         factor_t[last - 1] = turn(gate_psum, value[GATE_O, last - 1])
-        cell_t[last] = turn(spare_psum, cell[last])
-        squash(last - 1, whole(last - 1))
-        finish(last - 1, whole(last - 1), factor_t[last - 1])
-        pieces = [slice(0, BANK - LAST_PIECE), slice(BANK - LAST_PIECE, BANK)]
-        turned = []
-        for cols, pool in zip(pieces, (gate_psum, gate_psum)):
+        cell_t[last] = turn(gate_psum, cell[last])
+        finish(last - 1, whole, factor_t[last - 1])
+        last_factors = []
+        for cols in halves:
             activate(GATE_O, last, cols)
-            turned.append(turn(pool, value[GATE_O, last][:, cols]))
-        for cols, factor_cols in zip(pieces, turned):
-            squash(last, cols)
+            last_factors.append(turn(gate_psum, value[GATE_O, last][:, cols]))
+        for cols, factor_cols in zip(halves, last_factors):
             finish(last, cols, factor_cols)

import math
from contextlib import ExitStack

import concourse.mybir as mybir
from concourse.masks import make_identity

B, D, H = 1024, 512, 1024
FLOPS = 2 * B * D * 3 * H
BYTES = B * D * 2 + 3 * H * (D // 2 + D // 32) + 2 * 3 * H * 2 + B * H * 4

F32 = mybir.dt.float32
BF16 = mybir.dt.bfloat16
I32 = mybir.dt.int32
U32 = mybir.dt.uint32
U8 = mybir.dt.uint8
E5M2X4 = mybir.dt.float8_e5m2_x4
E2M1X4 = mybir.dt.float4_e2m1fn_x4
ACT = mybir.ActivationFunctionType
ALU = mybir.AluOpType

P = 128
BANK = 512
HALF = BANK // 2
TILES = H // P
WORD_BYTES = 2
GATE_I, GATE_G, GATE_O = 0, 1, 2
I_AND_G = slice(0, 3, 2)
O_ONLY = slice(3, 4)

EARLY_TILES = 3
RAMP_UNITS = 2
X_CHUNKS = ((0, 1), (1, 1), (2, 1), (3, 1), (4, 2), (6, 2))
X_LATE_STEP = 2

POLY_DEGREE = 8
POLY_UNITS = (3, 7, 10)
POLY_PACE = (6, 5, 5, 2)
GATE_BUFS = 4
RESULT_BUFS = 8


def tanh_over_c_coefficients(degree):
    count = degree + 1
    nodes = [0.5 - 0.5 * math.cos(math.pi * (k + 0.5) / count) for k in range(count)]
    diffs = [math.tanh(math.sqrt(u)) / math.sqrt(u) for u in nodes]
    for order in range(1, count):
        for k in range(degree, order - 1, -1):
            diffs[k] = (diffs[k] - diffs[k - 1]) / (nodes[k] - nodes[k - order])
    coeffs = [diffs[degree]]
    for k in range(degree - 1, -1, -1):
        coeffs = [low - nodes[k] * high for low, high in zip([0.0] + coeffs, coeffs + [0.0])]
        coeffs[0] += diffs[k]
    return coeffs


def tile_lstmbaseline_pa_kernel(tc, x, W_ih0_words, W_ih0_scales, b_ih0, b_hh0, out):
    nc = tc.nc
    units = [(j, t0) for t0 in (0, BANK) for j in range(TILES)]
    last = len(units) - 1
    whole = slice(0, BANK)
    halves = (slice(0, HALF), slice(HALF, BANK))
    coeffs = tanh_over_c_coefficients(POLY_DEGREE)

    with ExitStack() as ctx:
        keep = ctx.enter_context(tc.tile_pool(name="keep", bufs=1))
        work = ctx.enter_context(tc.tile_pool(name="work", bufs=GATE_BUFS))
        gate_psum = ctx.enter_context(tc.psum_pool(name="gate_psum", bufs=4))
        cell_psum = ctx.enter_context(tc.psum_pool(name="cell_psum", bufs=1))
        factor_psum = ctx.enter_context(tc.psum_pool(name="factor_psum", bufs=1))
        spare_psum = ctx.enter_context(tc.psum_pool(name="spare_psum", bufs=2))
        ctx.enter_context(tc.manual_schedule())

        ident = keep.tile([P, P], F32, align_bytes=64)
        pick = keep.tile([P, TILES], BF16, align_bytes=64)
        bias_rows = keep.tile([P, 3, P], BF16, align_bytes=64)
        bias_ig = keep.tile([P, 2, TILES], F32, align_bytes=64)
        bias_o = keep.tile([P, 1, TILES], F32, align_bytes=64)
        w_ig_early = keep.tile([P, 2, WORD_BYTES * P * EARLY_TILES], U8, align_bytes=64)
        w_ig_late = keep.tile([P, 2, WORD_BYTES * P * (TILES - EARLY_TILES)], U8, align_bytes=64)
        w_o = keep.tile([P, WORD_BYTES * H], U8, align_bytes=64)
        ws_ig = keep.tile([P, 2, H], U8, align_bytes=64)
        ws_o = keep.tile([P, H], U8, align_bytes=64)
        x_codes = keep.tile([P, B], U32, align_bytes=64)
        x_scales = keep.tile([P, B], U8, align_bytes=64)
        x_rows = [keep.tile([P, 2, D], BF16, align_bytes=64, name="x_rows%d" % n) for n in range(B // (2 * P))]

        words = W_ih0_words[0].rearrange("p (g n) -> p g n", g=4)
        scales = W_ih0_scales[0].rearrange("q (g n) -> q g n", g=4)

        x_turned, x_grouped = {}, {}

        def load_x(n):
            nc.sync.dma_start(out=x_rows[n][:], in_=x[2 * n * P:2 * (n + 1) * P, :].rearrange("(b p) k -> p b k", p=P))

        def turn_x(chunk, pool):
            first_block, blocks = X_CHUNKS[chunk]
            bank = pool.tile([P, BANK], F32, name="bank")
            x_turned[chunk] = bank[:, 0:blocks * 2 * P].rearrange("p (b u r) -> p b u r", b=blocks, u=2)
            for b in range(blocks):
                n, slot = divmod(first_block + b, 2)
                pairs = x_rows[n][:, slot, :].bitcast(F32)
                for u in range(2):
                    nc.tensor.transpose(x_turned[chunk][:, b, u, :], pairs[:, u:2 * P:2], ident[:])

        def group_x(chunk):
            blocks = X_CHUNKS[chunk][1]
            x_grouped[chunk] = keep.tile([P, blocks * 4 * P], BF16, align_bytes=64, name="x_grouped%d" % chunk)
            nc.vector.tensor_copy(
                out=x_grouped[chunk][:].bitcast(F32).rearrange("p (b r u) -> p b r u", b=blocks, u=2),
                in_=x_turned[chunk].rearrange("p b u r -> p b r u"),
            )

        def quantize_x(chunk):
            first_block, blocks = X_CHUNKS[chunk]
            tokens = slice(first_block * P, (first_block + blocks) * P)
            nc.vector.quantize_mx(out=x_codes[:, tokens].bitcast(E5M2X4), scales=x_scales[:, tokens], in_=x_grouped[chunk][:])

        def load_bias(queue, places, slots):
            for n, vector in enumerate((b_ih0, b_hh0)):
                rows = vector.rearrange("(g j c) -> j g c", g=4, c=P)
                queue.dma_start(out=bias_rows[n * TILES:(n + 1) * TILES, slots, :], in_=rows[:, places, :])

        def sum_bias(gates, dest):
            bank = factor_psum.tile([P, BANK], F32, name="bank")
            for n, gate in enumerate(gates):
                nc.tensor.matmul(bank[:, n * TILES:(n + 1) * TILES], lhsT=bias_rows[:, gate, :], rhs=pick[:], start=True, stop=True)
            nc.vector.tensor_copy(out=dest[:].rearrange("p g j -> p (g j)"), in_=bank[:, 0:len(gates) * TILES])

        sums, value = {}, {}
        cell, square, factor = {}, {}, {}
        cell_t, factor_t, tanh_c = {}, {}, {}
        horner = {}

        def fresh(tag, width, bufs=GATE_BUFS):
            tile = work.tile([P, BANK], F32, tag=tag, name=tag, bufs=bufs)
            return tile[:, 0:width]

        def multiply(gate, s, cols=whole):
            j, t0 = units[s]
            if gate == GATE_O:
                codes, first_tile, plane = w_o[:, :], 0, ws_o[:, P * j:P * (j + 1)]
            elif j < EARLY_TILES:
                codes, first_tile, plane = w_ig_early[:, gate, :], 0, ws_ig[:, gate, P * j:P * (j + 1)]
            else:
                codes, first_tile, plane = w_ig_late[:, gate, :], EARLY_TILES, ws_ig[:, gate, P * j:P * (j + 1)]
            codes = codes[:, WORD_BYTES * P * (j - first_tile):WORD_BYTES * P * (j - first_tile + 1)]
            if cols.start == 0:
                bank = gate_psum.tile([P, BANK], F32, name="bank")
                sums[gate, s] = bank[:, :]
            tokens = slice(t0 + cols.start, t0 + cols.stop)
            nc.tensor.matmul_mx(
                out=sums[gate, s][:, cols],
                lhsT=codes.bitcast(E2M1X4), lhsT_scale=plane,
                rhs=x_codes[:, tokens].bitcast(E5M2X4), rhs_scale=x_scales[:, tokens],
                start=True, stop=True,
            )

        def activate(gate, s, cols=whole):
            j = units[s][0]
            bias = bias_o[:, 0, j:j + 1] if gate == GATE_O else bias_ig[:, gate, j:j + 1]
            if cols.start == 0:
                value[gate, s] = fresh("gate%d" % gate, BANK)
            nc.scalar.activation(out=value[gate, s][:, cols], in_=sums[gate, s][:, cols],
                                 func=ACT.Tanh if gate == GATE_G else ACT.Sigmoid, bias=bias)

        def product(engine, tag, a, b):
            result = fresh(tag, BANK)
            engine.tensor_tensor(out=result, in0=a, in1=b, op=ALU.mult)
            return result

        def turn(pool, src):
            width = src.shape[1]
            bank = pool.tile([P, BANK], F32, name="bank")
            for b in range(width // P):
                nc.tensor.transpose(bank[:, b * P:(b + 1) * P], src[:, b * P:(b + 1) * P], ident[:])
            return bank[:, 0:width]

        def store(s, cols, result):
            j, t0 = units[s]
            nc.sync.dma_start(
                out=out[t0 + cols.start:t0 + cols.stop, j * P:(j + 1) * P].rearrange("(b p) c -> p b c", p=P),
                in_=result.rearrange("p (b c) -> p b c", c=P),
            )

        def finish(s, cols, factor_cols):
            width = cols.stop - cols.start
            tanh_c[s] = fresh("tanh_c", width)
            nc.scalar.activation(out=tanh_c[s], in_=cell_t[s][:, cols], func=ACT.Tanh)
            result = fresh("result", width, RESULT_BUFS)
            nc.vector.tensor_tensor(out=result, in0=factor_cols, in1=tanh_c[s], op=ALU.mult)
            store(s, cols, result)

        def horner_step(s, index):
            k, half = divmod(index, 2)
            u = cell_t[s][:, halves[half]]
            if k == 0:
                acc = fresh("horner", HALF)
                nc.vector.tensor_scalar(out=acc, in0=u, scalar1=coeffs[POLY_DEGREE], scalar2=coeffs[POLY_DEGREE - 1],
                                        op0=ALU.mult, op1=ALU.add)
            elif k == 1:
                acc = fresh("horner", HALF)
                nc.vector.tensor_tensor(out=acc, in0=u, in1=horner[half], op=ALU.mult)
            elif k < POLY_DEGREE:
                acc = fresh("horner", HALF)
                nc.vector.scalar_tensor_tensor(out=acc, in0=horner[half], scalar=coeffs[POLY_DEGREE - k], in1=u,
                                               op0=ALU.add, op1=ALU.mult)
            else:
                acc = fresh("result", HALF, RESULT_BUFS)
                nc.vector.scalar_tensor_tensor(out=acc, in0=horner[half], scalar=coeffs[0], in1=factor_t[s][:, halves[half]],
                                               op0=ALU.add, op1=ALU.mult)
                store(s, halves[half], acc)
            horner[half] = acc

        nc.vector.memset(bias_rows[:], 0.0)
        nc.vector.memset(ident[:], 0.0)
        early_bytes = WORD_BYTES * P * EARLY_TILES
        load_x(0)
        load_bias(nc.sync, I_AND_G, slice(GATE_I, GATE_O))
        load_x(1)
        for r in range(4):
            nc.sync.dma_start(out=ws_ig[r:P:32, :, :].bitcast(I32), in_=scales[r:16:4, I_AND_G, :].bitcast(I32))
        make_identity(nc, ident[:], nomemset=True)
        nc.gpsimd.dma_start(out=w_ig_early[:].bitcast(I32), in_=words[:, I_AND_G, 0:early_bytes].bitcast(I32))
        load_bias(nc.gpsimd, O_ONLY, slice(GATE_O, GATE_O + 1))
        nc.sync.dma_start(out=w_o[:].bitcast(I32), in_=words[:, O_ONLY.start, :].bitcast(I32))
        for r in range(4):
            nc.sync.dma_start(out=ws_o[r:P:32, :].bitcast(I32), in_=scales[r:16:4, O_ONLY.start, :].bitcast(I32))
        nc.sync.dma_start(out=w_ig_late[:].bitcast(I32), in_=words[:, I_AND_G, early_bytes:WORD_BYTES * H].bitcast(I32))
        load_x(2)
        load_x(3)
        nc.vector.tensor_tensor(out=pick[:], in0=ident[:, 0:TILES], in1=ident[:, TILES:2 * TILES], op=ALU.add)

        turn_x(0, spare_psum)
        turn_x(1, spare_psum)
        group_x(0)
        group_x(1)
        quantize_x(0)
        turn_x(2, cell_psum)
        quantize_x(1)
        sum_bias((GATE_I, GATE_G), bias_ig)
        group_x(2)
        turn_x(3, spare_psum)
        group_x(3)
        quantize_x(2)
        quantize_x(3)

        ramp = [(gate, s) for s in range(RAMP_UNITS) for gate in (GATE_I, GATE_G)]
        for gate, s in ramp:
            multiply(gate, s, halves[0])
        for gate, s in ramp:
            activate(gate, s, halves[0])
        for gate, s in ramp:
            multiply(gate, s, halves[1])
        sum_bias((GATE_O,), bias_o)
        for (gate, s), following in zip(ramp, ((GATE_O, 0), (GATE_I, 2), (GATE_G, 2), (GATE_O, 1))):
            activate(gate, s, halves[1])
            multiply(*following)
            if gate == GATE_G:
                cell[s] = product(nc.gpsimd, "cell", value[GATE_I, s], value[GATE_G, s])
        activate(GATE_O, 0)
        cell_t[0] = turn(cell_psum, cell[0])

        for s in range(RAMP_UNITS, last + 1):
            activate(GATE_I, s)
            if s < last:
                multiply(GATE_I, s + 1)
                multiply(GATE_G, s + 1)
            activate(GATE_G, s)
            cell[s] = product(nc.vector if s == last else nc.gpsimd, "cell", value[GATE_I, s], value[GATE_G, s])
            if s in POLY_UNITS:
                square[s] = product(nc.gpsimd, "square", cell[s], cell[s])
            multiply(GATE_O, s)
            late = s - X_LATE_STEP
            if late in (1, 2):
                quantize_x(3 + late)
            if late in (0, 1):
                turn_x(4 + late, spare_psum)
                group_x(4 + late)
            if s - 3 in POLY_UNITS:
                factor_t[s - 3] = turn(spare_psum, factor[s - 3])
            for poly in POLY_UNITS:
                age = s - 2 - poly
                if 0 <= age < len(POLY_PACE):
                    for index in range(sum(POLY_PACE[:age]), sum(POLY_PACE[:age + 1])):
                        horner_step(poly, index)
            activate(GATE_O, s - 1)
            if s - 1 in POLY_UNITS:
                factor[s - 1] = product(nc.gpsimd, "factor", value[GATE_O, s - 1], cell[s - 1])
            if s == last:
                cell_t[s - 1] = turn(spare_psum, cell[s - 1])
            if s - 2 not in POLY_UNITS:
                factor_t[s - 2] = turn(factor_psum, value[GATE_O, s - 2])
                finish(s - 2, whole, factor_t[s - 2])
            if s - 1 in POLY_UNITS:
                cell_t[s - 1] = turn(spare_psum, square[s - 1])
            elif s < last:
                cell_t[s - 1] = turn(cell_psum, cell[s - 1])

        factor_t[last - 1] = turn(gate_psum, value[GATE_O, last - 1])
        cell_t[last] = turn(gate_psum, cell[last])
        finish(last - 1, whole, factor_t[last - 1])
        last_factors = []
        for cols in halves:
            activate(GATE_O, last, cols)
            last_factors.append(turn(gate_psum, value[GATE_O, last][:, cols]))
        for cols, factor_cols in zip(halves, last_factors):
            finish(last, cols, factor_cols)
